import numpy as np
import ml_dtypes


def mxq(x, axis, fmt="e4m3"):
    dtype, down = {"e4m3": (ml_dtypes.float8_e4m3fn, 7), "e5m2": (ml_dtypes.float8_e5m2, 14)}[fmt]
    v = np.moveaxis(np.asarray(x, np.float32).astype(ml_dtypes.bfloat16).astype(np.float64), axis, -1)
    blocks = v.reshape(v.shape[:-1] + (-1, 32))
    amax = np.abs(blocks).max(-1, keepdims=True)
    byte = np.maximum(np.where(amax > 0, np.frexp(amax)[1] - 1 + 127, 0) - down, 1)
    scale = np.exp2(byte - 127.0)
    codes = (blocks / scale).astype(np.float32).astype(dtype).astype(np.float64)
    return np.moveaxis((codes * scale).reshape(v.shape), -1, axis)


WIDE = False


def mx_kscale(k):
    if not WIDE:
        return np.ones(k)
    levels = np.array([20, -20, 10, -10, 0])
    a = np.random.permutation(np.resize(levels, k // 512 * 4)).reshape(k // 512, 4)
    idx = np.arange(k)
    return np.exp2(a[idx // 512, idx % 128 // 32])


BF16 = ml_dtypes.bfloat16


def bf(x):
    return np.asarray(x, np.float32).astype(BF16)


def f64(x):
    return np.asarray(x).astype(np.float64)


M, J, L, H, K, I, S = 2, 1024, 32, 32, 3, 512, 2
SHIFT = 1


def setup_inputs():
    u = mx_kscale(I)
    x = np.random.standard_normal((M, J, L, H))
    w1 = np.random.standard_normal((I, S))
    w2 = np.random.standard_normal((J, K, I)) / np.sqrt(J * K) / u[None, None, :]
    g = (np.random.standard_normal((M, I, L, H)) * np.exp2(np.random.randint(-12, 1, (M, 1, L, H)))
         * 4.0 * u[None, :, None, None])
    return {"x": bf(x.reshape(M, J * L, H)), "w1": bf(w1), "w2": bf(w2), "grad_out": bf(g)}


def reference(x, w1, w2, grad_out):
    g = f64(grad_out).transpose(0, 2, 3, 1)
    v = f64(w1)
    d = np.roll(g, -1, axis=1) * v[:, 0] + np.roll(g, -2, axis=1) * v[:, 1]
    dq = mxq(d.reshape(M * L * H, I), 1, "e5m2")
    wq = mxq(f64(w2).reshape(J * K, I), 1, "e4m3")
    z = (dq @ wq.T).reshape(M, L, H, J, K)
    zp = np.pad(z, ((0, 0), (0, 0), (1, 1), (0, 0), (0, 0)))
    dx = sum(zp[:, :, 2 - k:2 - k + H, :, k] for k in range(K))
    return dx.transpose(0, 3, 1, 2).reshape(M, J * L, H)

@@ -1,0 +1,231 @@
+from contextlib import ExitStack
+
+import concourse.masks as masks
+import concourse.mybir as mybir
+
+FLOPS = 2 * 2048 * 3072 * 512
+BYTES = 512 * 2 * 2 + 1024 * 3 * 512 * 2 + 2 * 512 * 1024 * 2 + 2 * 32768 * 32 * 4
+
+F32 = mybir.dt.float32
+BF16 = mybir.dt.bfloat16
+U32 = mybir.dt.uint32
+U8 = mybir.dt.uint8
+E4M3 = mybir.dt.float8_e4m3fn_x4
+E5M2 = mybir.dt.float8_e5m2_x4
+MULT = mybir.AluOpType.mult
+ADD = mybir.AluOpType.add
+COPY = mybir.ActivationFunctionType.Copy
+
+P = 128
+D_PATH = ("pe", "vs")
+OUT_ENG = ((("v", "s"), ("s", "s")), (("v", "s"), ("v", "s")))
+
+
+def tile_kernel_generated_1_t_kernel(tc, x, w1, w2, grad_out, out):
+    nc = tc.nc
+    with ExitStack() as ctx:
+        keep = ctx.enter_context(tc.tile_pool(name="keep", bufs=1))
+        outs = ctx.enter_context(tc.tile_pool(name="outs", bufs=8))
+        psum = ctx.enter_context(tc.psum_pool(name="psum", bufs=8))
+
+        g_sb = [keep.tile([P, 4, 1088], BF16, name="g_sb%d" % m) for m in range(2)]
+        w2_sb = keep.tile([P, 12288], BF16, name="w2_sb")
+        w1_bf = keep.tile([P, 8], BF16, name="w1_bf")
+        w1_f = keep.tile([P, 8], F32, name="w1_f")
+        ident_f = keep.tile([P, P], F32, name="ident_f")
+        ident_b = keep.tile([P, P], BF16, name="ident_b")
+        diag = keep.tile([P, 8, P], BF16, name="diag")
+        dg = [keep.tile([P, 4352], BF16, name="dg%d" % m, align_bytes=64) for m in range(2)]
+        da_c = [keep.tile([P, 1024], U32, name="da_c%d" % m, align_bytes=64) for m in range(2)]
+        da_s = [keep.tile([P, 1024], U8, name="da_s%d" % m, align_bytes=64) for m in range(2)]
+        db_c = [keep.tile([P, 1088], U32, name="db_c%d" % m, align_bytes=64) for m in range(2)]
+        db_s = [keep.tile([P, 1088], U8, name="db_s%d" % m, align_bytes=64) for m in range(2)]
+        wg = keep.tile([P, 12288], BF16, name="wg", align_bytes=64)
+        wc = keep.tile([P, 3072], U32, name="wc", align_bytes=64)
+        ws = keep.tile([P, 3072], U8, name="ws", align_bytes=64)
+        tmp = keep.tile([P, 4, 1024], F32, name="tmp")
+        dn = keep.tile([P, 4, 1024], BF16, name="dn")
+
+        w2_f = w2_sb[:].bitcast(F32)
+        wg_f = wg[:].bitcast(F32)
+
+        def evac(eng, dst, src):
+            if eng == "v":
+                nc.vector.tensor_copy(out=dst, in_=src)
+            else:
+                nc.scalar.copy(out=dst, in_=src)
+
+        def load_g(m):
+            for u in range(2):
+                nc.sync.dma_start(
+                    out=g_sb[m][:, 2 * u : 2 * u + 2, 0:1024],
+                    in_=grad_out[m, 256 * u : 256 * u + 256].rearrange("(p e) l n -> p e (l n)", e=2),
+                )
+
+        def load_w2(jp):
+            nc.sync.dma_start(
+                out=w2_sb[:, 3072 * jp : 3072 * jp + 3072].rearrange("j (a c) -> j a c", a=2),
+                in_=w2[256 * jp : 256 * jp + 256].rearrange("(a j) k i -> j a (k i)", a=2),
+            )
+
+        def wrap_g(m):
+            nc.vector.tensor_copy(out=g_sb[m][:, :, 1024:1088], in_=g_sb[m][:, :, 0:64])
+
+        def d_pe(m):
+            dg4 = dg[m][:, 128:4224].rearrange("p (n l t) -> p n l t", n=32, l=32)
+            for lc in range(8):
+                bank = psum.tile([P, 4, 128], F32, name="dbank", tag="bank")
+                for t in range(4):
+                    for s in range(2):
+                        c0 = (4 * lc + 1 + s) * 32
+                        nc.tensor.matmul(
+                            out=bank[:, t, :],
+                            lhsT=diag[:, 2 * t + s, :],
+                            rhs=g_sb[m][:, t, c0 : c0 + 128],
+                            start=(s == 0),
+                            stop=(s == 1),
+                        )
+                evac(
+                    "v" if lc % 2 == 0 else "s",
+                    dg4[:, :, 4 * lc : 4 * lc + 4, :],
+                    bank[:].rearrange("p t (l n) -> p n l t", l=4),
+                )
+
+        def d_vs_tmp(m, t):
+            nc.scalar.activation(
+                out=tmp[:, t, :], in_=g_sb[m][:, t, 64:1088], func=COPY, scale=w1_f[:, 2 * t + 1 : 2 * t + 2]
+            )
+
+        def d_vs_sum(m, t):
+            nc.vector.scalar_tensor_tensor(
+                out=dn[:, t, :],
+                in0=g_sb[m][:, t, 32:1056],
+                scalar=w1_f[:, 2 * t : 2 * t + 1],
+                in1=tmp[:, t, :],
+                op0=MULT,
+                op1=ADD,
+            )
+
+        def d_vs_regroup(m, hn):
+            dst = dg[m][:, 128:4224].rearrange("p (q i l t) -> p q l t i", q=8, i=4, l=32)
+            src = dn[:].rearrange("p t (l q i) -> p q l t i", l=32, q=8)
+            nc.vector.tensor_copy(out=dst[:, 4 * hn : 4 * hn + 4], in_=src[:, 4 * hn : 4 * hn + 4])
+
+        def quant(codes, scales, src, col, width, fmt):
+            nc.vector.quantize_mx(
+                out=codes[:, col : col + width].bitcast(fmt),
+                scales=scales[:, col : col + width],
+                in_=src,
+            )
+
+        def quant_d(m, piece):
+            if piece == 0:
+                quant(da_c[m], da_s[m], dg[m][:, 128:2176], 0, 512, E5M2)
+            elif piece == 1:
+                quant(db_c[m], db_s[m], dg[m][:, 0:2048], 0, 512, E5M2)
+            elif piece == 2:
+                quant(db_c[m], db_s[m], dg[m][:, 2048:4096], 512, 512, E5M2)
+            elif piece == 3:
+                quant(da_c[m], da_s[m], dg[m][:, 2176:4224], 512, 512, E5M2)
+            else:
+                quant(db_c[m], db_s[m], dg[m][:, 4096:4352], 1024, 64, E5M2)
+
+        def transposes(jp):
+            for bk in range(3):
+                c0 = 6 * jp + 2 * bk
+                bank = psum.tile([P, 2, 2, 128], F32, name="xbank", tag="bank")
+                for cc in range(2):
+                    for u in range(2):
+                        w0 = 256 * (c0 + cc) + 128 * u
+                        nc.tensor.transpose(bank[:, cc, u, :], w2_f[:, w0 : w0 + 128], ident_f[:])
+                evac(
+                    "s",
+                    wg_f[:, 256 * c0 : 256 * c0 + 512].rearrange("p (c j u) -> p c j u", c=2, u=2),
+                    bank[:].rearrange("p c u j -> p c j u"),
+                )
+
+        def quant_w(jp):
+            quant(wc, ws, wg[:, 3072 * jp : 3072 * jp + 2048], 768 * jp, 512, E4M3)
+            quant(wc, ws, wg[:, 3072 * jp + 2048 : 3072 * jp + 3072], 768 * jp + 512, 256, E4M3)
+
+        def mx(m, jt):
+            o_sb = outs.tile([P, 1024], F32, name="o_sb")
+            o3 = o_sb[:].rearrange("j (l p) -> j l p", p=32)
+            for h in range(2):
+                acc = psum.tile([P, 512], F32, name="acc", tag="bank")
+                taps = (
+                    (1, da_c[m], da_s[m], 512 * h),
+                    (2, db_c[m], db_s[m], 512 * h),
+                    (0, db_c[m], db_s[m], 512 * h + 64),
+                )
+                for idx, (k, codes, scales, col) in enumerate(taps):
+                    wcol = (3 * jt + k) * 128
+                    nc.tensor.matmul_mx(
+                        out=acc[:],
+                        lhsT=wc[:, wcol : wcol + 128].bitcast(E4M3),
+                        lhsT_scale=ws[:, wcol : wcol + 128],
+                        rhs=codes[:, col : col + 512].bitcast(E5M2),
+                        rhs_scale=scales[:, col : col + 512],
+                        start=(idx == 0),
+                        stop=(idx == 2),
+                    )
+                evac(
+                    OUT_ENG[m][jt % 2][h],
+                    o3[:, :, 16 * h : 16 * h + 16],
+                    acc[:].rearrange("j (r l) -> j l r", l=32),
+                )
+            nc.sync.dma_start(
+                out=out[m, 4096 * jt : 4096 * jt + 4096, :].rearrange("(j l) p -> j (l p)", l=32),
+                in_=o_sb[:],
+            )
+
+        nc.scalar.dma_start(
+            out=w1_bf[:].rearrange("p (u c) -> p u c", u=2),
+            in_=w1.rearrange("(u p e) s -> p u (e s)", u=2, e=2),
+        )
+        load_g(0)
+        load_w2(0)
+        load_w2(1)
+        load_g(1)
+        load_w2(2)
+        load_w2(3)
+
+        masks.make_identity(nc, ident_f[:])
+        nc.vector.tensor_copy(out=ident_b[:], in_=ident_f[:])
+        nc.vector.tensor_copy(out=w1_f[:], in_=w1_bf[:])
+        for c in range(8):
+            nc.vector.tensor_scalar(
+                out=diag[:, c, :], in0=ident_b[:], scalar1=w1_f[:, c : c + 1], scalar2=None, op0=MULT
+            )
+        for m in range(2):
+            nc.vector.memset(dg[m][:, 0:128], 0.0)
+            nc.vector.memset(dg[m][:, 4224:4352], 0.0)
+
+        wrap_g(0)
+        d_pe(0)
+        transposes(0)
+        for piece in range(3):
+            quant_d(0, piece)
+        quant_w(0)
+        transposes(1)
+        for piece in range(3, 5):
+            quant_d(0, piece)
+        quant_w(1)
+        wrap_g(1)
+
+        background = [
+            [lambda: d_vs_tmp(1, 0), lambda: d_vs_tmp(1, 1), lambda: d_vs_sum(1, 0)],
+            [lambda: d_vs_tmp(1, 2), lambda: d_vs_tmp(1, 3), lambda: d_vs_sum(1, 1), lambda: d_vs_sum(1, 2)],
+            [lambda: d_vs_sum(1, 3), lambda: d_vs_regroup(1, 0), lambda: d_vs_regroup(1, 1)],
+            [lambda: quant_d(1, 0), lambda: quant_d(1, 1), lambda: quant_d(1, 2), lambda: quant_d(1, 3), lambda: quant_d(1, 4)],
+        ]
+        for jp in range(4):
+            mx(0, 2 * jp)
+            mx(0, 2 * jp + 1)
+            if jp + 2 < 4:
+                transposes(jp + 2)
+                quant_w(jp + 2)
+            for step in background[jp]:
+                step()
+        for jt in range(8):
+            mx(1, jt)

@@ -17,8 +17,10 @@ ADD = mybir.AluOpType.add
 COPY = mybir.ActivationFunctionType.Copy
 
 P = 128
-D_PATH = ("pe", "vs")
-OUT_ENG = ((("v", "s"), ("s", "s")), (("v", "s"), ("v", "s")))
+OUT_ENG = (
+    (("v", "v"), ("v", "v"), ("v", "s"), ("s", "s"), ("s", "s"), ("s", "s"), ("s", "s"), ("s", "s")),
+    (("v", "s"),) * 8,
+)
 
 
 def tile_kernel_generated_1_t_kernel(tc, x, w1, w2, grad_out, out):
@@ -55,11 +57,11 @@ def tile_kernel_generated_1_t_kernel(tc, x, w1, w2, grad_out, out):
             else:
                 nc.scalar.copy(out=dst, in_=src)
 
-        def load_g(m):
+        def load_g(m, l0, l1):
             for u in range(2):
                 nc.sync.dma_start(
-                    out=g_sb[m][:, 2 * u : 2 * u + 2, 0:1024],
-                    in_=grad_out[m, 256 * u : 256 * u + 256].rearrange("(p e) l n -> p e (l n)", e=2),
+                    out=g_sb[m][:, 2 * u : 2 * u + 2, 32 * l0 : 32 * l1],
+                    in_=grad_out[m, 256 * u : 256 * u + 256, l0:l1].rearrange("(p e) l n -> p e (l n)", e=2),
                 )
 
         def load_w2(jp):
@@ -71,25 +73,20 @@ def tile_kernel_generated_1_t_kernel(tc, x, w1, w2, grad_out, out):
         def wrap_g(m):
             nc.vector.tensor_copy(out=g_sb[m][:, :, 1024:1088], in_=g_sb[m][:, :, 0:64])
 
-        def d_pe(m):
+        def d_pe(m, lc, eng):
             dg4 = dg[m][:, 128:4224].rearrange("p (n l t) -> p n l t", n=32, l=32)
-            for lc in range(8):
-                bank = psum.tile([P, 4, 128], F32, name="dbank", tag="bank")
-                for t in range(4):
-                    for s in range(2):
-                        c0 = (4 * lc + 1 + s) * 32
-                        nc.tensor.matmul(
-                            out=bank[:, t, :],
-                            lhsT=diag[:, 2 * t + s, :],
-                            rhs=g_sb[m][:, t, c0 : c0 + 128],
-                            start=(s == 0),
-                            stop=(s == 1),
-                        )
-                evac(
-                    "v" if lc % 2 == 0 else "s",
-                    dg4[:, :, 4 * lc : 4 * lc + 4, :],
-                    bank[:].rearrange("p t (l n) -> p n l t", l=4),
-                )
+            bank = psum.tile([P, 4, 128], F32, name="dbank", tag="bank")
+            for t in range(4):
+                for s in range(2):
+                    c0 = (4 * lc + 1 + s) * 32
+                    nc.tensor.matmul(
+                        out=bank[:, t, :],
+                        lhsT=diag[:, 2 * t + s, :],
+                        rhs=g_sb[m][:, t, c0 : c0 + 128],
+                        start=(s == 0),
+                        stop=(s == 1),
+                    )
+            evac(eng, dg4[:, :, 4 * lc : 4 * lc + 4, :], bank[:].rearrange("p t (l n) -> p n l t", l=4))
 
         def d_vs_tmp(m, t):
             nc.scalar.activation(
@@ -119,34 +116,31 @@ def tile_kernel_generated_1_t_kernel(tc, x, w1, w2, grad_out, out):
             )
 
         def quant_d(m, piece):
-            if piece == 0:
+            if piece == "A0":
                 quant(da_c[m], da_s[m], dg[m][:, 128:2176], 0, 512, E5M2)
-            elif piece == 1:
-                quant(db_c[m], db_s[m], dg[m][:, 0:2048], 0, 512, E5M2)
-            elif piece == 2:
-                quant(db_c[m], db_s[m], dg[m][:, 2048:4096], 512, 512, E5M2)
-            elif piece == 3:
+            elif piece == "A1":
                 quant(da_c[m], da_s[m], dg[m][:, 2176:4224], 512, 512, E5M2)
+            elif piece == "B0":
+                quant(db_c[m], db_s[m], dg[m][:, 0:2048], 0, 512, E5M2)
+            elif piece == "Bm":
+                quant(db_c[m], db_s[m], dg[m][:, 2048:2304], 512, 64, E5M2)
             else:
-                quant(db_c[m], db_s[m], dg[m][:, 4096:4352], 1024, 64, E5M2)
+                quant(db_c[m], db_s[m], dg[m][:, 2304:4352], 576, 512, E5M2)
 
-        def transposes(jp):
-            for bk in range(3):
-                c0 = 6 * jp + 2 * bk
-                bank = psum.tile([P, 2, 2, 128], F32, name="xbank", tag="bank")
-                for cc in range(2):
-                    for u in range(2):
-                        w0 = 256 * (c0 + cc) + 128 * u
-                        nc.tensor.transpose(bank[:, cc, u, :], w2_f[:, w0 : w0 + 128], ident_f[:])
-                evac(
-                    "s",
-                    wg_f[:, 256 * c0 : 256 * c0 + 512].rearrange("p (c j u) -> p c j u", c=2, u=2),
-                    bank[:].rearrange("p c u j -> p c j u"),
-                )
+        def transposes(c0):
+            bank = psum.tile([P, 2, 2, 128], F32, name="xbank", tag="bank")
+            for cc in range(2):
+                for u in range(2):
+                    w0 = 256 * (c0 + cc) + 128 * u
+                    nc.tensor.transpose(bank[:, cc, u, :], w2_f[:, w0 : w0 + 128], ident_f[:])
+            evac(
+                "s",
+                wg_f[:, 256 * c0 : 256 * c0 + 512].rearrange("p (c j u) -> p c j u", c=2, u=2),
+                bank[:].rearrange("p c u j -> p c j u"),
+            )
 
-        def quant_w(jp):
-            quant(wc, ws, wg[:, 3072 * jp : 3072 * jp + 2048], 768 * jp, 512, E4M3)
-            quant(wc, ws, wg[:, 3072 * jp + 2048 : 3072 * jp + 3072], 768 * jp + 512, 256, E4M3)
+        def quant_w(c0, n):
+            quant(wc, ws, wg[:, 512 * c0 : 512 * (c0 + n)], 128 * c0, 128 * n, E4M3)
 
         def mx(m, jt):
             o_sb = outs.tile([P, 1024], F32, name="o_sb")
@@ -170,7 +164,7 @@ def tile_kernel_generated_1_t_kernel(tc, x, w1, w2, grad_out, out):
                         stop=(idx == 2),
                     )
                 evac(
-                    OUT_ENG[m][jt % 2][h],
+                    OUT_ENG[m][jt][h],
                     o3[:, :, 16 * h : 16 * h + 16],
                     acc[:].rearrange("j (r l) -> j l r", l=32),
                 )
@@ -179,15 +173,18 @@ def tile_kernel_generated_1_t_kernel(tc, x, w1, w2, grad_out, out):
                 in_=o_sb[:],
             )
 
+        ctx.enter_context(tc.manual_schedule())
+
         nc.scalar.dma_start(
             out=w1_bf[:].rearrange("p (u c) -> p u c", u=2),
             in_=w1.rearrange("(u p e) s -> p u (e s)", u=2, e=2),
         )
-        load_g(0)
+        load_g(0, 0, 10)
+        load_g(0, 10, 32)
         load_w2(0)
         load_w2(1)
-        load_g(1)
         load_w2(2)
+        load_g(1, 0, 32)
         load_w2(3)
 
         masks.make_identity(nc, ident_f[:])
@@ -202,30 +199,47 @@ def tile_kernel_generated_1_t_kernel(tc, x, w1, w2, grad_out, out):
             nc.vector.memset(dg[m][:, 4224:4352], 0.0)
 
         wrap_g(0)
-        d_pe(0)
-        transposes(0)
-        for piece in range(3):
+        for lc in range(5):
+            d_pe(0, lc, "v" if lc % 2 == 0 else "s")
+        for c0 in (0, 2, 4):
+            transposes(c0)
+        for lc in range(5, 8):
+            d_pe(0, lc, "v" if lc % 2 == 0 else "s")
+        quant_w(0, 4)
+        for c0 in (6, 8, 10):
+            transposes(c0)
+        for piece in ("A0", "B0", "Bm"):
             quant_d(0, piece)
-        quant_w(0)
-        transposes(1)
-        for piece in range(3, 5):
+        for c0 in (12, 14, 16):
+            transposes(c0)
+        for piece in ("A1", "B1"):
             quant_d(0, piece)
-        quant_w(1)
+        quant_w(4, 2)
         wrap_g(1)
 
-        background = [
-            [lambda: d_vs_tmp(1, 0), lambda: d_vs_tmp(1, 1), lambda: d_vs_sum(1, 0)],
-            [lambda: d_vs_tmp(1, 2), lambda: d_vs_tmp(1, 3), lambda: d_vs_sum(1, 1), lambda: d_vs_sum(1, 2)],
-            [lambda: d_vs_sum(1, 3), lambda: d_vs_regroup(1, 0), lambda: d_vs_regroup(1, 1)],
-            [lambda: quant_d(1, 0), lambda: quant_d(1, 1), lambda: quant_d(1, 2), lambda: quant_d(1, 3), lambda: quant_d(1, 4)],
-        ]
-        for jp in range(4):
-            mx(0, 2 * jp)
-            mx(0, 2 * jp + 1)
-            if jp + 2 < 4:
-                transposes(jp + 2)
-                quant_w(jp + 2)
-            for step in background[jp]:
+        background = (
+            (lambda: d_vs_tmp(1, 0), lambda: quant_w(6, 4), lambda: d_vs_tmp(1, 1), lambda: quant_w(10, 2)),
+            (
+                lambda: d_vs_tmp(1, 2),
+                lambda: d_vs_sum(1, 0),
+                lambda: d_vs_tmp(1, 3),
+                lambda: d_vs_sum(1, 1),
+                lambda: quant_w(12, 4),
+                lambda: quant_w(16, 2),
+            ),
+            (lambda: d_vs_sum(1, 2), lambda: d_vs_sum(1, 3)),
+            (lambda: quant_w(18, 4), lambda: quant_w(22, 2), lambda: d_vs_regroup(1, 0)),
+            (lambda: d_vs_regroup(1, 1),),
+            (lambda: quant_d(1, "A0"), lambda: quant_d(1, "B0")),
+            (lambda: quant_d(1, "Bm"), lambda: quant_d(1, "B1")),
+            (lambda: quant_d(1, "A1"),),
+        )
+        for jt in range(8):
+            mx(0, jt)
+            if jt == 2:
+                for c0 in (18, 20, 22):
+                    transposes(c0)
+            for step in background[jt]:
                 step()
         for jt in range(8):
             mx(1, jt)

@@ -17,6 +17,7 @@ ADD = mybir.AluOpType.add
 COPY = mybir.ActivationFunctionType.Copy
 
 P = 128
+N_WARM = 6
 OUT_ENG = (
     (("v", "v"), ("v", "v"), ("v", "s"), ("s", "s"), ("s", "s"), ("s", "s"), ("s", "s"), ("s", "s")),
     (("v", "s"),) * 8,
@@ -47,6 +48,7 @@ def tile_kernel_generated_1_t_kernel(tc, x, w1, w2, grad_out, out):
         ws = keep.tile([P, 3072], U8, name="ws", align_bytes=64)
         tmp = keep.tile([P, 4, 1024], F32, name="tmp")
         dn = keep.tile([P, 4, 1024], BF16, name="dn")
+        zeros = keep.tile([P, 512], BF16, name="zeros")
 
         w2_f = w2_sb[:].bitcast(F32)
         wg_f = wg[:].bitcast(F32)
@@ -186,6 +188,11 @@ def tile_kernel_generated_1_t_kernel(tc, x, w1, w2, grad_out, out):
         load_w2(2)
         load_g(1, 0, 32)
         load_w2(3)
+
+        nc.vector.memset(zeros[:], 0.0)
+        warm = psum.tile([P, 512], F32, name="warm", tag="bank")
+        for rep in range(N_WARM):
+            nc.tensor.matmul(out=warm[:], lhsT=zeros[:, 0:128], rhs=zeros[:], start=True, stop=True)
 
         masks.make_identity(nc, ident_f[:])
         nc.vector.tensor_copy(out=ident_b[:], in_=ident_f[:])

@@ -17,7 +17,6 @@ ADD = mybir.AluOpType.add
 COPY = mybir.ActivationFunctionType.Copy
 
 P = 128
-N_WARM = 6
 OUT_ENG = (
     (("v", "v"), ("v", "v"), ("v", "s"), ("s", "s"), ("s", "s"), ("s", "s"), ("s", "s"), ("s", "s")),
     (("v", "s"),) * 8,
@@ -48,7 +47,6 @@ def tile_kernel_generated_1_t_kernel(tc, x, w1, w2, grad_out, out):
         ws = keep.tile([P, 3072], U8, name="ws", align_bytes=64)
         tmp = keep.tile([P, 4, 1024], F32, name="tmp")
         dn = keep.tile([P, 4, 1024], BF16, name="dn")
-        zeros = keep.tile([P, 512], BF16, name="zeros")
 
         w2_f = w2_sb[:].bitcast(F32)
         wg_f = wg[:].bitcast(F32)
@@ -105,10 +103,10 @@ def tile_kernel_generated_1_t_kernel(tc, x, w1, w2, grad_out, out):
                 op1=ADD,
             )
 
-        def d_vs_regroup(m, hn):
+        def d_vs_regroup(m, q0, q1):
             dst = dg[m][:, 128:4224].rearrange("p (q i l t) -> p q l t i", q=8, i=4, l=32)
             src = dn[:].rearrange("p t (l q i) -> p q l t i", l=32, q=8)
-            nc.vector.tensor_copy(out=dst[:, 4 * hn : 4 * hn + 4], in_=src[:, 4 * hn : 4 * hn + 4])
+            nc.vector.tensor_copy(out=dst[:, q0:q1], in_=src[:, q0:q1])
 
         def quant(codes, scales, src, col, width, fmt):
             nc.vector.quantize_mx(
@@ -144,36 +142,48 @@ def tile_kernel_generated_1_t_kernel(tc, x, w1, w2, grad_out, out):
         def quant_w(c0, n):
             quant(wc, ws, wg[:, 512 * c0 : 512 * (c0 + n)], 128 * c0, 128 * n, E4M3)
 
-        def mx(m, jt):
-            o_sb = outs.tile([P, 1024], F32, name="o_sb")
+        o_tiles = {}
+
+        def mxh(m, jt, h, eng, cuts=1):
+            if (m, jt) not in o_tiles:
+                o_tiles[(m, jt)] = [outs.tile([P, 1024], F32, name="o_sb"), 0]
+            o_sb = o_tiles[(m, jt)][0]
             o3 = o_sb[:].rearrange("j (l p) -> j l p", p=32)
-            for h in range(2):
-                acc = psum.tile([P, 512], F32, name="acc", tag="bank")
-                taps = (
-                    (1, da_c[m], da_s[m], 512 * h),
-                    (2, db_c[m], db_s[m], 512 * h),
-                    (0, db_c[m], db_s[m], 512 * h + 64),
-                )
-                for idx, (k, codes, scales, col) in enumerate(taps):
-                    wcol = (3 * jt + k) * 128
-                    nc.tensor.matmul_mx(
-                        out=acc[:],
-                        lhsT=wc[:, wcol : wcol + 128].bitcast(E4M3),
-                        lhsT_scale=ws[:, wcol : wcol + 128],
-                        rhs=codes[:, col : col + 512].bitcast(E5M2),
-                        rhs_scale=scales[:, col : col + 512],
-                        start=(idx == 0),
-                        stop=(idx == 2),
-                    )
-                evac(
-                    OUT_ENG[m][jt][h],
-                    o3[:, :, 16 * h : 16 * h + 16],
-                    acc[:].rearrange("j (r l) -> j l r", l=32),
-                )
-            nc.sync.dma_start(
-                out=out[m, 4096 * jt : 4096 * jt + 4096, :].rearrange("(j l) p -> j (l p)", l=32),
-                in_=o_sb[:],
+            o_dram = out[m, 4096 * jt : 4096 * jt + 4096, :].rearrange("(j l) p -> j (l p)", l=32)
+            acc = psum.tile([P, 512], F32, name="acc", tag="bank")
+            taps = (
+                (1, da_c[m], da_s[m], 512 * h),
+                (2, db_c[m], db_s[m], 512 * h),
+                (0, db_c[m], db_s[m], 512 * h + 64),
             )
+            for idx, (k, codes, scales, col) in enumerate(taps):
+                wcol = (3 * jt + k) * 128
+                nc.tensor.matmul_mx(
+                    out=acc[:],
+                    lhsT=wc[:, wcol : wcol + 128].bitcast(E4M3),
+                    lhsT_scale=ws[:, wcol : wcol + 128],
+                    rhs=codes[:, col : col + 512].bitcast(E5M2),
+                    rhs_scale=scales[:, col : col + 512],
+                    start=(idx == 0),
+                    stop=(idx == 2),
+                )
+            o_tiles[(m, jt)][1] += 1
+            nl = 32 // cuts
+            for cut in range(cuts):
+                evac(
+                    eng,
+                    o3[:, nl * cut : nl * (cut + 1), 16 * h : 16 * h + 16],
+                    acc[:].rearrange("j (r l) -> j l r", l=32)[:, nl * cut : nl * (cut + 1), :],
+                )
+                if o_tiles[(m, jt)][1] == 2:
+                    nc.sync.dma_start(
+                        out=o_dram[:, 32 * nl * cut : 32 * nl * (cut + 1)],
+                        in_=o_sb[:, 32 * nl * cut : 32 * nl * (cut + 1)],
+                    )
+
+        def mx(m, jt):
+            for h in range(2):
+                mxh(m, jt, h, OUT_ENG[m][jt][h])
 
         ctx.enter_context(tc.manual_schedule())
 
@@ -188,11 +198,6 @@ def tile_kernel_generated_1_t_kernel(tc, x, w1, w2, grad_out, out):
         load_w2(2)
         load_g(1, 0, 32)
         load_w2(3)
-
-        nc.vector.memset(zeros[:], 0.0)
-        warm = psum.tile([P, 512], F32, name="warm", tag="bank")
-        for rep in range(N_WARM):
-            nc.tensor.matmul(out=warm[:], lhsT=zeros[:, 0:128], rhs=zeros[:], start=True, stop=True)
 
         masks.make_identity(nc, ident_f[:])
         nc.vector.tensor_copy(out=ident_b[:], in_=ident_f[:])
@@ -235,10 +240,10 @@ def tile_kernel_generated_1_t_kernel(tc, x, w1, w2, grad_out, out):
                 lambda: quant_w(16, 2),
             ),
             (lambda: d_vs_sum(1, 2), lambda: d_vs_sum(1, 3)),
-            (lambda: quant_w(18, 4), lambda: quant_w(22, 2), lambda: d_vs_regroup(1, 0)),
-            (lambda: d_vs_regroup(1, 1),),
-            (lambda: quant_d(1, "A0"), lambda: quant_d(1, "B0")),
-            (lambda: quant_d(1, "Bm"), lambda: quant_d(1, "B1")),
+            (lambda: quant_w(18, 4), lambda: quant_w(22, 2), lambda: d_vs_regroup(1, 0, 6)),
+            (lambda: quant_d(1, "A0"),),
+            (lambda: quant_d(1, "B0"), lambda: quant_d(1, "Bm")),
+            (lambda: d_vs_regroup(1, 6, 8),),
             (lambda: quant_d(1, "A1"),),
         )
         for jt in range(8):
@@ -248,5 +253,13 @@ def tile_kernel_generated_1_t_kernel(tc, x, w1, w2, grad_out, out):
                     transposes(c0)
             for step in background[jt]:
                 step()
-        for jt in range(8):
-            mx(1, jt)
+        mxh(1, 0, 0, "s")
+        quant_d(1, "B1")
+        mxh(1, 1, 0, "s")
+        mxh(1, 2, 0, "s")
+        mxh(1, 0, 1, "s")
+        mxh(1, 1, 1, "v")
+        mxh(1, 2, 1, "s")
+        for jt in range(3, 8):
+            mxh(1, jt, 0, "v")
+            mxh(1, jt, 1, "s", cuts=(2 if jt == 7 else 1))

@@ -9,6 +9,7 @@ BYTES = 512 * 2 * 2 + 1024 * 3 * 512 * 2 + 2 * 512 * 1024 * 2 + 2 * 32768 * 32 *
 F32 = mybir.dt.float32
 BF16 = mybir.dt.bfloat16
 U32 = mybir.dt.uint32
+I32 = mybir.dt.int32
 U8 = mybir.dt.uint8
 E4M3 = mybir.dt.float8_e4m3fn_x4
 E5M2 = mybir.dt.float8_e5m2_x4
@@ -17,10 +18,14 @@ ADD = mybir.AluOpType.add
 COPY = mybir.ActivationFunctionType.Copy
 
 P = 128
-OUT_ENG = (
-    (("v", "v"), ("v", "v"), ("v", "s"), ("s", "s"), ("s", "s"), ("s", "s"), ("s", "s"), ("s", "s")),
-    (("v", "s"),) * 8,
-)
+LAG = 2
+S_RATE = 2
+V_RATE = 1
+T_RUNS = {1: (12, 14, 16), 3: (18, 20, 22)}
+
+
+def vector_copies_out(u):
+    return u in (0, 1) or (u >= 8 and u % 3 == 2) or (u >= 24 and u % 2 == 0)
 
 
 def tile_kernel_generated_1_t_kernel(tc, x, w1, w2, grad_out, out):
@@ -37,16 +42,14 @@ def tile_kernel_generated_1_t_kernel(tc, x, w1, w2, grad_out, out):
         ident_f = keep.tile([P, P], F32, name="ident_f")
         ident_b = keep.tile([P, P], BF16, name="ident_b")
         diag = keep.tile([P, 8, P], BF16, name="diag")
-        dg = [keep.tile([P, 4352], BF16, name="dg%d" % m, align_bytes=64) for m in range(2)]
-        da_c = [keep.tile([P, 1024], U32, name="da_c%d" % m, align_bytes=64) for m in range(2)]
-        da_s = [keep.tile([P, 1024], U8, name="da_s%d" % m, align_bytes=64) for m in range(2)]
-        db_c = [keep.tile([P, 1088], U32, name="db_c%d" % m, align_bytes=64) for m in range(2)]
-        db_s = [keep.tile([P, 1088], U8, name="db_s%d" % m, align_bytes=64) for m in range(2)]
+        dg = [keep.tile([P, 2048], BF16, name="dg%d" % c, align_bytes=64) for c in range(4)]
+        dc = keep.tile([P, 4 * 544], U32, name="dc", align_bytes=64)
+        sp = keep.tile([P, 4 * 1536], U8, name="sp", align_bytes=64)
         wg = keep.tile([P, 12288], BF16, name="wg", align_bytes=64)
         wc = keep.tile([P, 3072], U32, name="wc", align_bytes=64)
         ws = keep.tile([P, 3072], U8, name="ws", align_bytes=64)
-        tmp = keep.tile([P, 4, 1024], F32, name="tmp")
-        dn = keep.tile([P, 4, 1024], BF16, name="dn")
+        tmp = {c: keep.tile([P, 4, 512], F32, name="tmp%d" % c) for c in (1, 2, 3)}
+        dn = {c: keep.tile([P, 4, 512], BF16, name="dn%d" % c) for c in (1, 2, 3)}
 
         w2_f = w2_sb[:].bitcast(F32)
         wg_f = wg[:].bitcast(F32)
@@ -73,12 +76,13 @@ def tile_kernel_generated_1_t_kernel(tc, x, w1, w2, grad_out, out):
         def wrap_g(m):
             nc.vector.tensor_copy(out=g_sb[m][:, :, 1024:1088], in_=g_sb[m][:, :, 0:64])
 
-        def d_pe(m, lc, eng):
-            dg4 = dg[m][:, 128:4224].rearrange("p (n l t) -> p n l t", n=32, l=32)
+        def d_pe(c, b, eng):
+            m, lh = divmod(c, 2)
+            dg4 = dg[c][:].rearrange("p (n l t) -> p n l t", n=32, l=16)
             bank = psum.tile([P, 4, 128], F32, name="dbank", tag="bank")
             for t in range(4):
                 for s in range(2):
-                    c0 = (4 * lc + 1 + s) * 32
+                    c0 = (16 * lh + 4 * b + 1 + s) * 32
                     nc.tensor.matmul(
                         out=bank[:, t, :],
                         lhsT=diag[:, 2 * t + s, :],
@@ -86,104 +90,102 @@ def tile_kernel_generated_1_t_kernel(tc, x, w1, w2, grad_out, out):
                         start=(s == 0),
                         stop=(s == 1),
                     )
-            evac(eng, dg4[:, :, 4 * lc : 4 * lc + 4, :], bank[:].rearrange("p t (l n) -> p n l t", l=4))
+            evac(eng, dg4[:, :, 4 * b : 4 * b + 4, :], bank[:].rearrange("p t (l n) -> p n l t", l=4))
 
-        def d_vs_tmp(m, t):
+        def d_tmp(c, t):
+            m, lh = divmod(c, 2)
+            c0 = (16 * lh + 2) * 32
             nc.scalar.activation(
-                out=tmp[:, t, :], in_=g_sb[m][:, t, 64:1088], func=COPY, scale=w1_f[:, 2 * t + 1 : 2 * t + 2]
+                out=tmp[c][:, t, :], in_=g_sb[m][:, t, c0 : c0 + 512], func=COPY, scale=w1_f[:, 2 * t + 1 : 2 * t + 2]
             )
 
-        def d_vs_sum(m, t):
+        def d_sum(c, t):
+            m, lh = divmod(c, 2)
+            c0 = (16 * lh + 1) * 32
             nc.vector.scalar_tensor_tensor(
-                out=dn[:, t, :],
-                in0=g_sb[m][:, t, 32:1056],
+                out=dn[c][:, t, :],
+                in0=g_sb[m][:, t, c0 : c0 + 512],
                 scalar=w1_f[:, 2 * t : 2 * t + 1],
-                in1=tmp[:, t, :],
+                in1=tmp[c][:, t, :],
                 op0=MULT,
                 op1=ADD,
             )
 
-        def d_vs_regroup(m, q0, q1):
-            dst = dg[m][:, 128:4224].rearrange("p (q i l t) -> p q l t i", q=8, i=4, l=32)
-            src = dn[:].rearrange("p t (l q i) -> p q l t i", l=32, q=8)
-            nc.vector.tensor_copy(out=dst[:, q0:q1], in_=src[:, q0:q1])
+        def d_regroup(c, half):
+            dst = dg[c][:].rearrange("p (q i l t) -> p q l t i", q=8, i=4, l=16)
+            src = dn[c][:].rearrange("p t (l q i) -> p q l t i", l=16, q=8)
+            nc.vector.tensor_copy(out=dst[:, 4 * half : 4 * half + 4], in_=src[:, 4 * half : 4 * half + 4])
 
-        def quant(codes, scales, src, col, width, fmt):
+        def quant_d(c):
             nc.vector.quantize_mx(
-                out=codes[:, col : col + width].bitcast(fmt),
-                scales=scales[:, col : col + width],
-                in_=src,
+                out=dc[:, 544 * c + 16 : 544 * c + 528].bitcast(E5M2),
+                scales=sp[:, 1536 * c + 512 : 1536 * c + 1024],
+                in_=dg[c][:],
             )
 
-        def quant_d(m, piece):
-            if piece == "A0":
-                quant(da_c[m], da_s[m], dg[m][:, 128:2176], 0, 512, E5M2)
-            elif piece == "A1":
-                quant(da_c[m], da_s[m], dg[m][:, 2176:4224], 512, 512, E5M2)
-            elif piece == "B0":
-                quant(db_c[m], db_s[m], dg[m][:, 0:2048], 0, 512, E5M2)
-            elif piece == "Bm":
-                quant(db_c[m], db_s[m], dg[m][:, 2048:2304], 512, 64, E5M2)
-            else:
-                quant(db_c[m], db_s[m], dg[m][:, 2304:4352], 576, 512, E5M2)
+        def planes(c):
+            b0 = 1536 * c
+            nc.vector.tensor_copy(
+                out=sp[:, b0 : b0 + 496].bitcast(I32), in_=sp[:, b0 + 528 : b0 + 1024].bitcast(I32)
+            )
+            nc.vector.tensor_copy(
+                out=sp[:, b0 + 1040 : b0 + 1536].bitcast(I32), in_=sp[:, b0 + 512 : b0 + 1008].bitcast(I32)
+            )
 
-        def transposes(c0):
+        banks = {}
+
+        def t_pe(c0):
             bank = psum.tile([P, 2, 2, 128], F32, name="xbank", tag="bank")
             for cc in range(2):
                 for u in range(2):
                     w0 = 256 * (c0 + cc) + 128 * u
                     nc.tensor.transpose(bank[:, cc, u, :], w2_f[:, w0 : w0 + 128], ident_f[:])
+            banks[("T", c0)] = bank
+
+        def t_ev(c0):
             evac(
                 "s",
                 wg_f[:, 256 * c0 : 256 * c0 + 512].rearrange("p (c j u) -> p c j u", c=2, u=2),
-                bank[:].rearrange("p c u j -> p c j u"),
+                banks[("T", c0)][:].rearrange("p c u j -> p c j u"),
             )
 
         def quant_w(c0, n):
-            quant(wc, ws, wg[:, 512 * c0 : 512 * (c0 + n)], 128 * c0, 128 * n, E4M3)
-
-        o_tiles = {}
-
-        def mxh(m, jt, h, eng, cuts=1):
-            if (m, jt) not in o_tiles:
-                o_tiles[(m, jt)] = [outs.tile([P, 1024], F32, name="o_sb"), 0]
-            o_sb = o_tiles[(m, jt)][0]
-            o3 = o_sb[:].rearrange("j (l p) -> j l p", p=32)
-            o_dram = out[m, 4096 * jt : 4096 * jt + 4096, :].rearrange("(j l) p -> j (l p)", l=32)
-            acc = psum.tile([P, 512], F32, name="acc", tag="bank")
-            taps = (
-                (1, da_c[m], da_s[m], 512 * h),
-                (2, db_c[m], db_s[m], 512 * h),
-                (0, db_c[m], db_s[m], 512 * h + 64),
+            nc.vector.quantize_mx(
+                out=wc[:, 128 * c0 : 128 * (c0 + n)].bitcast(E4M3),
+                scales=ws[:, 128 * c0 : 128 * (c0 + n)],
+                in_=wg[:, 512 * c0 : 512 * (c0 + n)],
             )
-            for idx, (k, codes, scales, col) in enumerate(taps):
+
+        def unit_pe(c, jt):
+            acc = psum.tile([P, 512], F32, name="acc", tag="bank")
+            for idx, k in enumerate((1, 0, 2)):
                 wcol = (3 * jt + k) * 128
+                col = 544 * c + 16 * (2 - k)
                 nc.tensor.matmul_mx(
                     out=acc[:],
                     lhsT=wc[:, wcol : wcol + 128].bitcast(E4M3),
                     lhsT_scale=ws[:, wcol : wcol + 128],
-                    rhs=codes[:, col : col + 512].bitcast(E5M2),
-                    rhs_scale=scales[:, col : col + 512],
+                    rhs=dc[:, col : col + 512].bitcast(E5M2),
+                    rhs_scale=sp[:, 1536 * c + 512 * k : 1536 * c + 512 * k + 512],
                     start=(idx == 0),
                     stop=(idx == 2),
                 )
-            o_tiles[(m, jt)][1] += 1
-            nl = 32 // cuts
-            for cut in range(cuts):
-                evac(
-                    eng,
-                    o3[:, nl * cut : nl * (cut + 1), 16 * h : 16 * h + 16],
-                    acc[:].rearrange("j (r l) -> j l r", l=32)[:, nl * cut : nl * (cut + 1), :],
-                )
-                if o_tiles[(m, jt)][1] == 2:
-                    nc.sync.dma_start(
-                        out=o_dram[:, 32 * nl * cut : 32 * nl * (cut + 1)],
-                        in_=o_sb[:, 32 * nl * cut : 32 * nl * (cut + 1)],
-                    )
+            banks[("U", c, jt)] = acc
 
-        def mx(m, jt):
-            for h in range(2):
-                mxh(m, jt, h, OUT_ENG[m][jt][h])
+        def unit_ev(c, jt, eng, cuts):
+            m, lh = divmod(c, 2)
+            acc = banks[("U", c, jt)]
+            o_sb = outs.tile([P, 512], F32, name="o_sb")
+            o3 = o_sb[:].rearrange("j (l p) -> j l p", p=32)
+            a3 = acc[:].rearrange("j (p l) -> j l p", l=16)
+            o_dram = out[m, 4096 * jt : 4096 * jt + 4096, :].rearrange("(j l) p -> j (l p)", l=32)
+            nl = 16 // cuts
+            for cut in range(cuts):
+                evac(eng, o3[:, nl * cut : nl * (cut + 1), :], a3[:, nl * cut : nl * (cut + 1), :])
+                nc.sync.dma_start(
+                    out=o_dram[:, 512 * lh + 32 * nl * cut : 512 * lh + 32 * nl * (cut + 1)],
+                    in_=o_sb[:, 32 * nl * cut : 32 * nl * (cut + 1)],
+                )
 
         ctx.enter_context(tc.manual_schedule())
 
@@ -192,13 +194,19 @@ def tile_kernel_generated_1_t_kernel(tc, x, w1, w2, grad_out, out):
             in_=w1.rearrange("(u p e) s -> p u (e s)", u=2, e=2),
         )
         load_g(0, 0, 10)
-        load_g(0, 10, 32)
+        load_g(0, 10, 18)
+        load_g(0, 18, 32)
         load_w2(0)
         load_w2(1)
         load_w2(2)
-        load_g(1, 0, 32)
         load_w2(3)
+        load_g(1, 0, 18)
+        load_g(1, 18, 32)
 
+        nc.vector.memset(sp[:].bitcast(I32), 0)
+        dc_i = dc[:].bitcast(I32).rearrange("p (c w) -> p c w", c=4)
+        nc.vector.memset(dc_i[:, :, 0:16], 0)
+        nc.vector.memset(dc_i[:, :, 528:544], 0)
         masks.make_identity(nc, ident_f[:])
         nc.vector.tensor_copy(out=ident_b[:], in_=ident_f[:])
         nc.vector.tensor_copy(out=w1_f[:], in_=w1_bf[:])
@@ -206,60 +214,101 @@ def tile_kernel_generated_1_t_kernel(tc, x, w1, w2, grad_out, out):
             nc.vector.tensor_scalar(
                 out=diag[:, c, :], in0=ident_b[:], scalar1=w1_f[:, c : c + 1], scalar2=None, op0=MULT
             )
-        for m in range(2):
-            nc.vector.memset(dg[m][:, 0:128], 0.0)
-            nc.vector.memset(dg[m][:, 4224:4352], 0.0)
 
         wrap_g(0)
-        for lc in range(5):
-            d_pe(0, lc, "v" if lc % 2 == 0 else "s")
+        d_pe(0, 0, "s")
+        d_pe(0, 1, "v")
+        d_tmp(1, 0)
+        d_pe(0, 2, "s")
+        d_sum(1, 0)
+        d_pe(0, 3, "v")
+        d_tmp(1, 1)
         for c0 in (0, 2, 4):
-            transposes(c0)
-        for lc in range(5, 8):
-            d_pe(0, lc, "v" if lc % 2 == 0 else "s")
-        quant_w(0, 4)
+            t_pe(c0)
+        quant_d(0)
+        planes(0)
+        for c0 in (0, 2, 4):
+            t_ev(c0)
+        d_sum(1, 1)
         for c0 in (6, 8, 10):
-            transposes(c0)
-        for piece in ("A0", "B0", "Bm"):
-            quant_d(0, piece)
-        for c0 in (12, 14, 16):
-            transposes(c0)
-        for piece in ("A1", "B1"):
-            quant_d(0, piece)
+            t_pe(c0)
+        quant_w(0, 4)
         quant_w(4, 2)
-        wrap_g(1)
 
-        background = (
-            (lambda: d_vs_tmp(1, 0), lambda: quant_w(6, 4), lambda: d_vs_tmp(1, 1), lambda: quant_w(10, 2)),
-            (
-                lambda: d_vs_tmp(1, 2),
-                lambda: d_vs_sum(1, 0),
-                lambda: d_vs_tmp(1, 3),
-                lambda: d_vs_sum(1, 1),
-                lambda: quant_w(12, 4),
-                lambda: quant_w(16, 2),
-            ),
-            (lambda: d_vs_sum(1, 2), lambda: d_vs_sum(1, 3)),
-            (lambda: quant_w(18, 4), lambda: quant_w(22, 2), lambda: d_vs_regroup(1, 0, 6)),
-            (lambda: quant_d(1, "A0"),),
-            (lambda: quant_d(1, "B0"), lambda: quant_d(1, "Bm")),
-            (lambda: d_vs_regroup(1, 6, 8),),
-            (lambda: quant_d(1, "A1"),),
-        )
-        for jt in range(8):
-            mx(0, jt)
-            if jt == 2:
-                for c0 in (18, 20, 22):
-                    transposes(c0)
-            for step in background[jt]:
-                step()
-        mxh(1, 0, 0, "s")
-        quant_d(1, "B1")
-        mxh(1, 1, 0, "s")
-        mxh(1, 2, 0, "s")
-        mxh(1, 0, 1, "s")
-        mxh(1, 1, 1, "v")
-        mxh(1, 2, 1, "s")
-        for jt in range(3, 8):
-            mxh(1, jt, 0, "v")
-            mxh(1, jt, 1, "s", cuts=(2 if jt == 7 else 1))
+        def s_chain(c, ts):
+            need = (("wrap", 1),) if c == 3 else ()
+            return [(("tmp", c, t), need, lambda c=c, t=t: d_tmp(c, t)) for t in ts]
+
+        def s_tev(c0s):
+            return [(("tev", c0), (), lambda c0=c0: t_ev(c0)) for c0 in c0s]
+
+        def v_sums(c, ts):
+            return [(("sum", c, t), (("tmp", c, t),), lambda c=c, t=t: d_sum(c, t)) for t in ts]
+
+        def v_finish(c):
+            return [
+                (("rg", c, 0), (), lambda c=c: d_regroup(c, 0)),
+                (("rg", c, 1), (), lambda c=c: d_regroup(c, 1)),
+                (("qd", c), (), lambda c=c: quant_d(c)),
+                (("pl", c), (), lambda c=c: planes(c)),
+            ]
+
+        def v_qw(jp):
+            return [
+                (("qw", 6 * jp), (("tev", 6 * jp + 2),), lambda jp=jp: quant_w(6 * jp, 4)),
+                (("qw", 6 * jp + 4), (("tev", 6 * jp + 4),), lambda jp=jp: quant_w(6 * jp + 4, 2)),
+            ]
+
+        streams = {
+            "s": s_tev((6, 8, 10)) + s_chain(1, (2, 3)) + s_tev((12, 14, 16, 18, 20, 22)) + s_chain(2, range(4)) + s_chain(3, range(4)),
+            "v": v_qw(1) + v_sums(1, (2, 3)) + v_qw(2) + v_finish(1)[0:2] + v_qw(3) + v_finish(1)[2:4]
+            + [(("wrap", 1), (), lambda: wrap_g(1))]
+            + v_sums(2, range(4)) + v_finish(2) + v_sums(3, range(4)) + v_finish(3),
+        }
+        pos = {"s": 0, "v": 0}
+        written = set()
+        t_written = set((0, 2, 4, 6, 8, 10))
+
+        def step(q):
+            if pos[q] >= len(streams[q]):
+                return False
+            label, needs, call = streams[q][pos[q]]
+            for need in (label,) + tuple(needs):
+                if need[0] == "tev" and need[1] not in t_written:
+                    return False
+            for need in needs:
+                flush("v" if q == "s" else "s", need)
+            pos[q] = pos[q] + 1
+            call()
+            written.add(label)
+            return True
+
+        def flush(q, label):
+            while label not in written:
+                assert step(q)
+
+        units = [(c, jt) for c in range(4) for jt in range(8)]
+        copied = {"n": 0}
+
+        def copy_out_up_to(last):
+            while copied["n"] <= last:
+                u = copied["n"]
+                unit_ev(units[u][0], units[u][1], "v" if vector_copies_out(u) else "s", 2 if u == 31 else 1)
+                copied["n"] = u + 1
+
+        for u in range(32):
+            c, jt = units[u]
+            if jt >= 2:
+                flush("v", ("qw", 6 * (jt // 2) + 4))
+            if c >= 1:
+                flush("v", ("pl", c))
+            unit_pe(c, jt)
+            copy_out_up_to(u - LAG)
+            for c0 in T_RUNS.get(u, ()):
+                t_pe(c0)
+                t_written.add(c0)
+            for i in range(S_RATE):
+                step("s")
+            for i in range(V_RATE):
+                step("v")
+        copy_out_up_to(31)

@@ -18,14 +18,8 @@ ADD = mybir.AluOpType.add
 COPY = mybir.ActivationFunctionType.Copy
 
 P = 128
-LAG = 2
-S_RATE = 2
-V_RATE = 1
-T_RUNS = {1: (12, 14, 16), 3: (18, 20, 22)}
-
-
-def vector_copies_out(u):
-    return u in (0, 1) or (u >= 8 and u % 3 == 2) or (u >= 24 and u % 2 == 0)
+S_TMP = ()
+V_OUT = (1, 26, 28, 30)
 
 
 def tile_kernel_generated_1_t_kernel(tc, x, w1, w2, grad_out, out):
@@ -53,6 +47,7 @@ def tile_kernel_generated_1_t_kernel(tc, x, w1, w2, grad_out, out):
 
         w2_f = w2_sb[:].bitcast(F32)
         wg_f = wg[:].bitcast(F32)
+        banks = {}
 
         def evac(eng, dst, src):
             if eng == "v":
@@ -76,9 +71,8 @@ def tile_kernel_generated_1_t_kernel(tc, x, w1, w2, grad_out, out):
         def wrap_g(m):
             nc.vector.tensor_copy(out=g_sb[m][:, :, 1024:1088], in_=g_sb[m][:, :, 0:64])
 
-        def d_pe(c, b, eng):
+        def d_pe(c, b):
             m, lh = divmod(c, 2)
-            dg4 = dg[c][:].rearrange("p (n l t) -> p n l t", n=32, l=16)
             bank = psum.tile([P, 4, 128], F32, name="dbank", tag="bank")
             for t in range(4):
                 for s in range(2):
@@ -90,14 +84,27 @@ def tile_kernel_generated_1_t_kernel(tc, x, w1, w2, grad_out, out):
                         start=(s == 0),
                         stop=(s == 1),
                     )
-            evac(eng, dg4[:, :, 4 * b : 4 * b + 4, :], bank[:].rearrange("p t (l n) -> p n l t", l=4))
+            banks[("D", c, b)] = bank
 
-        def d_tmp(c, t):
+        def d_ev(c, b, eng):
+            dg4 = dg[c][:].rearrange("p (n l t) -> p n l t", n=32, l=16)
+            evac(eng, dg4[:, :, 4 * b : 4 * b + 4, :], banks[("D", c, b)][:].rearrange("p t (l n) -> p n l t", l=4))
+
+        def d_tmp(c, t, eng):
             m, lh = divmod(c, 2)
             c0 = (16 * lh + 2) * 32
-            nc.scalar.activation(
-                out=tmp[c][:, t, :], in_=g_sb[m][:, t, c0 : c0 + 512], func=COPY, scale=w1_f[:, 2 * t + 1 : 2 * t + 2]
-            )
+            if eng == "s":
+                nc.scalar.activation(
+                    out=tmp[c][:, t, :], in_=g_sb[m][:, t, c0 : c0 + 512], func=COPY, scale=w1_f[:, 2 * t + 1 : 2 * t + 2]
+                )
+            else:
+                nc.vector.tensor_scalar(
+                    out=tmp[c][:, t, :],
+                    in0=g_sb[m][:, t, c0 : c0 + 512],
+                    scalar1=w1_f[:, 2 * t + 1 : 2 * t + 2],
+                    scalar2=None,
+                    op0=MULT,
+                )
 
         def d_sum(c, t):
             m, lh = divmod(c, 2)
@@ -132,8 +139,6 @@ def tile_kernel_generated_1_t_kernel(tc, x, w1, w2, grad_out, out):
                 out=sp[:, b0 + 1040 : b0 + 1536].bitcast(I32), in_=sp[:, b0 + 512 : b0 + 1008].bitcast(I32)
             )
 
-        banks = {}
-
         def t_pe(c0):
             bank = psum.tile([P, 2, 2, 128], F32, name="xbank", tag="bank")
             for cc in range(2):
@@ -142,9 +147,9 @@ def tile_kernel_generated_1_t_kernel(tc, x, w1, w2, grad_out, out):
                     nc.tensor.transpose(bank[:, cc, u, :], w2_f[:, w0 : w0 + 128], ident_f[:])
             banks[("T", c0)] = bank
 
-        def t_ev(c0):
+        def t_ev(c0, eng):
             evac(
-                "s",
+                eng,
                 wg_f[:, 256 * c0 : 256 * c0 + 512].rearrange("p (c j u) -> p c j u", c=2, u=2),
                 banks[("T", c0)][:].rearrange("p c u j -> p c j u"),
             )
@@ -215,100 +220,117 @@ def tile_kernel_generated_1_t_kernel(tc, x, w1, w2, grad_out, out):
                 out=diag[:, c, :], in0=ident_b[:], scalar1=w1_f[:, c : c + 1], scalar2=None, op0=MULT
             )
 
-        wrap_g(0)
-        d_pe(0, 0, "s")
-        d_pe(0, 1, "v")
-        d_tmp(1, 0)
-        d_pe(0, 2, "s")
-        d_sum(1, 0)
-        d_pe(0, 3, "v")
-        d_tmp(1, 1)
-        for c0 in (0, 2, 4):
-            t_pe(c0)
-        quant_d(0)
-        planes(0)
-        for c0 in (0, 2, 4):
-            t_ev(c0)
-        d_sum(1, 1)
-        for c0 in (6, 8, 10):
-            t_pe(c0)
-        quant_w(0, 4)
-        quant_w(4, 2)
+        def tmp_on(c, t):
+            return "s" if (c, t) in S_TMP else "v"
 
-        def s_chain(c, ts):
-            need = (("wrap", 1),) if c == 3 else ()
-            return [(("tmp", c, t), need, lambda c=c, t=t: d_tmp(c, t)) for t in ts]
+        def i_tmp(c, t):
+            return (("tmp", c, t), (("wrap", c // 2),) if c % 2 else (), lambda: d_tmp(c, t, tmp_on(c, t)))
 
-        def s_tev(c0s):
-            return [(("tev", c0), (), lambda c0=c0: t_ev(c0)) for c0 in c0s]
+        def i_sum(c, t):
+            return (("sum", c, t), (("tmp", c, t),), lambda: d_sum(c, t))
 
-        def v_sums(c, ts):
-            return [(("sum", c, t), (("tmp", c, t),), lambda c=c, t=t: d_sum(c, t)) for t in ts]
+        def i_rg(c, half):
+            return (("rg", c, half), tuple(("sum", c, t) for t in range(4)), lambda: d_regroup(c, half))
 
-        def v_finish(c):
-            return [
-                (("rg", c, 0), (), lambda c=c: d_regroup(c, 0)),
-                (("rg", c, 1), (), lambda c=c: d_regroup(c, 1)),
-                (("qd", c), (), lambda c=c: quant_d(c)),
-                (("pl", c), (), lambda c=c: planes(c)),
-            ]
+        def i_qd(c):
+            need = tuple(("ed", b) for b in range(4)) if c == 0 else (("rg", c, 0), ("rg", c, 1))
+            return (("qd", c), need, lambda: quant_d(c))
 
-        def v_qw(jp):
-            return [
-                (("qw", 6 * jp), (("tev", 6 * jp + 2),), lambda jp=jp: quant_w(6 * jp, 4)),
-                (("qw", 6 * jp + 4), (("tev", 6 * jp + 4),), lambda jp=jp: quant_w(6 * jp + 4, 2)),
-            ]
+        def i_pl(c):
+            return (("pl", c), (("qd", c),), lambda: planes(c))
 
-        streams = {
-            "s": s_tev((6, 8, 10)) + s_chain(1, (2, 3)) + s_tev((12, 14, 16, 18, 20, 22)) + s_chain(2, range(4)) + s_chain(3, range(4)),
-            "v": v_qw(1) + v_sums(1, (2, 3)) + v_qw(2) + v_finish(1)[0:2] + v_qw(3) + v_finish(1)[2:4]
-            + [(("wrap", 1), (), lambda: wrap_g(1))]
-            + v_sums(2, range(4)) + v_finish(2) + v_sums(3, range(4)) + v_finish(3),
+        def i_qw(c0, n):
+            return (("qw", c0), tuple(("et", e) for e in range(c0 - c0 % 2, c0 + n, 2)), lambda: quant_w(c0, n))
+
+        def i_wrap(m):
+            return (("wrap", m), (), lambda: wrap_g(m))
+
+        def i_d(b):
+            return (("d", b), (), lambda: d_pe(0, b))
+
+        def i_ed(b, eng):
+            return (("ed", b), (("d", b),), lambda: d_ev(0, b, eng))
+
+        def i_t(c0):
+            return (("t", c0), (), lambda: t_pe(c0))
+
+        def i_et(c0, eng):
+            return (("et", c0), (("t", c0),), lambda: t_ev(c0, eng))
+
+        def i_u(u):
+            c, jt = divmod(u, 8)
+            return (("u", u), (("pl", c), ("qw", 6 * (jt // 2)), ("qw", 6 * (jt // 2) + 4)), lambda: unit_pe(c, jt))
+
+        def i_eu(u):
+            eng = "v" if u in V_OUT else "s"
+            return (("eu", u), (("u", u),), lambda: unit_ev(u // 8, u % 8, eng, 2 if u == 31 else 1))
+
+        def front(c):
+            order = ((0, 0), (0, 1), (1, 0), (0, 2), (1, 1), (0, 3), (1, 2), (1, 3))
+            return [(i_sum(c, t) if kind else i_tmp(c, t)) for kind, t in order if kind or tmp_on(c, t) == "v"]
+
+        def qw_pair(jp):
+            return [i_qw(6 * jp, 4), i_qw(6 * jp + 4, 2)]
+
+        def weave(a, b):
+            both = []
+            for i in range(max(len(a), len(b))):
+                both.extend(a[i : i + 1])
+                both.extend(b[i : i + 1])
+            return both
+
+        queues = {
+            "pe": [i_d(b) for b in range(4)]
+            + [i_t(c0) for c0 in (0, 2, 4, 6, 8, 10)]
+            + [i_u(0), i_u(1)]
+            + [i_t(c0) for c0 in (12, 14, 16)]
+            + [i_u(2), i_u(3)]
+            + [i_t(c0) for c0 in (18, 20, 22)]
+            + [i_u(u) for u in range(4, 32)],
+            "s": [i_ed(b, "s") for b in range(4)]
+            + [i_et(c0, "s") for c0 in (0, 2, 4, 6, 8, 10)]
+            + [i_eu(0)]
+            + [i_et(c0, "s") for c0 in (12, 14, 16)]
+            + [i_eu(2)]
+            + [i_et(c0, "s") for c0 in (18, 20, 22)]
+            + [i_eu(u) for u in range(3, 32) if u not in V_OUT],
+            "v": [i_wrap(0)]
+            + front(1)[0:4]
+            + [i_qd(0), front(1)[4], i_pl(0), front(1)[5]]
+            + qw_pair(0)
+            + front(1)[6:8]
+            + qw_pair(1)
+            + [i_rg(1, 0), i_eu(1), i_rg(1, 1)]
+            + [i_qw(12, 4), i_qd(1), i_qw(16, 2), i_pl(1), i_wrap(1)]
+            + front(2)[0:2]
+            + qw_pair(3)
+            + front(2)[2:8]
+            + [i_rg(2, 0), i_rg(2, 1), front(3)[0], i_qd(2), front(3)[1], i_pl(2)]
+            + front(3)[2:8]
+            + [i_rg(3, 0), i_rg(3, 1), i_qd(3), i_pl(3)]
+            + [i_eu(u) for u in V_OUT if u > 1],
         }
-        pos = {"s": 0, "v": 0}
-        written = set()
-        t_written = set((0, 2, 4, 6, 8, 10))
 
-        def step(q):
-            if pos[q] >= len(streams[q]):
-                return False
-            label, needs, call = streams[q][pos[q]]
-            for need in (label,) + tuple(needs):
-                if need[0] == "tev" and need[1] not in t_written:
-                    return False
-            for need in needs:
-                flush("v" if q == "s" else "s", need)
-            pos[q] = pos[q] + 1
-            call()
-            written.add(label)
-            return True
-
-        def flush(q, label):
-            while label not in written:
-                assert step(q)
-
-        units = [(c, jt) for c in range(4) for jt in range(8)]
-        copied = {"n": 0}
-
-        def copy_out_up_to(last):
-            while copied["n"] <= last:
-                u = copied["n"]
-                unit_ev(units[u][0], units[u][1], "v" if vector_copies_out(u) else "s", 2 if u == 31 else 1)
-                copied["n"] = u + 1
-
-        for u in range(32):
-            c, jt = units[u]
-            if jt >= 2:
-                flush("v", ("qw", 6 * (jt // 2) + 4))
-            if c >= 1:
-                flush("v", ("pl", c))
-            unit_pe(c, jt)
-            copy_out_up_to(u - LAG)
-            for c0 in T_RUNS.get(u, ()):
-                t_pe(c0)
-                t_written.add(c0)
-            for i in range(S_RATE):
-                step("s")
-            for i in range(V_RATE):
-                step("v")
-        copy_out_up_to(31)
+        frees = {"d": "ed", "t": "et", "u": "eu"}
+        done = set()
+        filled = []
+        heads = {q: 0 for q in queues}
+        left = sum(len(queues[q]) for q in queues)
+        while left:
+            moved = 0
+            for q in ("pe", "s", "v"):
+                if heads[q] >= len(queues[q]):
+                    continue
+                label, needs, call = queues[q][heads[q]]
+                if any(need not in done for need in needs):
+                    continue
+                if q == "pe":
+                    if len(filled) >= 8 and filled[len(filled) - 8] not in done:
+                        continue
+                    filled.append((frees[label[0]],) + tuple(label[1:]))
+                call()
+                done.add(label)
+                heads[q] = heads[q] + 1
+                moved = moved + 1
+            assert moved, "the three orders wait for each other"
+            left = left - moved

@@ -282,29 +282,28 @@ def tile_kernel_generated_1_t_kernel(tc, x, w1, w2, grad_out, out):
         queues = {
             "pe": [i_d(b) for b in range(4)]
             + [i_t(c0) for c0 in (0, 2, 4, 6, 8, 10)]
-            + [i_u(0), i_u(1)]
+            + [i_u(0)]
             + [i_t(c0) for c0 in (12, 14, 16)]
-            + [i_u(2), i_u(3)]
+            + [i_u(1)]
             + [i_t(c0) for c0 in (18, 20, 22)]
-            + [i_u(u) for u in range(4, 32)],
+            + [i_u(u) for u in range(2, 32)],
             "s": [i_ed(b, "s") for b in range(4)]
-            + [i_et(c0, "s") for c0 in (0, 2, 4, 6, 8, 10)]
+            + [i_et(c0, "s") for c0 in (0, 2, 4, 6, 8, 10, 12, 14, 16)]
             + [i_eu(0)]
-            + [i_et(c0, "s") for c0 in (12, 14, 16)]
-            + [i_eu(2)]
             + [i_et(c0, "s") for c0 in (18, 20, 22)]
-            + [i_eu(u) for u in range(3, 32) if u not in V_OUT],
+            + [i_eu(u) for u in range(2, 32) if u not in V_OUT],
             "v": [i_wrap(0)]
             + front(1)[0:4]
             + [i_qd(0), front(1)[4], i_pl(0), front(1)[5]]
             + qw_pair(0)
             + front(1)[6:8]
             + qw_pair(1)
-            + [i_rg(1, 0), i_eu(1), i_rg(1, 1)]
-            + [i_qw(12, 4), i_qd(1), i_qw(16, 2), i_pl(1), i_wrap(1)]
-            + front(2)[0:2]
+            + [i_rg(1, 0)]
+            + qw_pair(2)
+            + [i_eu(1), i_rg(1, 1)]
             + qw_pair(3)
-            + front(2)[2:8]
+            + [i_qd(1), i_wrap(1), i_pl(1)]
+            + front(2)
             + [i_rg(2, 0), i_rg(2, 1), front(3)[0], i_qd(2), front(3)[1], i_pl(2)]
             + front(3)[2:8]
             + [i_rg(3, 0), i_rg(3, 1), i_qd(3), i_pl(3)]

@@ -177,6 +177,11 @@ def tile_kernel_generated_1_t_kernel(tc, x, w1, w2, grad_out, out):
                 )
             banks[("U", c, jt)] = acc
 
+        def warm_pe():
+            bank = psum.tile([P, 512], F32, name="warm", tag="bank")
+            for i in range(2):
+                nc.tensor.matmul(out=bank[:], lhsT=ident_b[:], rhs=g_sb[0][:, i, 0:512], start=True, stop=True)
+
         def unit_ev(c, jt, eng, cuts):
             m, lh = divmod(c, 2)
             acc = banks[("U", c, jt)]
@@ -261,6 +266,9 @@ def tile_kernel_generated_1_t_kernel(tc, x, w1, w2, grad_out, out):
             c, jt = divmod(u, 8)
             return (("u", u), (("pl", c), ("qw", 6 * (jt // 2)), ("qw", 6 * (jt // 2) + 4)), lambda: unit_pe(c, jt))
 
+        def i_x(n):
+            return (("x", n), (), warm_pe)
+
         def i_eu(u):
             eng = "v" if u in V_OUT else "s"
             return (("eu", u), (("u", u),), lambda: unit_ev(u // 8, u % 8, eng, 2 if u == 31 else 1))
@@ -281,7 +289,10 @@ def tile_kernel_generated_1_t_kernel(tc, x, w1, w2, grad_out, out):
 
         queues = {
             "pe": [i_d(b) for b in range(4)]
-            + [i_t(c0) for c0 in (0, 2, 4, 6, 8, 10)]
+            + [i_x(0)]
+            + [i_t(c0) for c0 in (0, 2, 4)]
+            + [i_x(1)]
+            + [i_t(c0) for c0 in (6, 8, 10)]
             + [i_u(0)]
             + [i_t(c0) for c0 in (12, 14, 16)]
             + [i_u(1)]
@@ -310,7 +321,7 @@ def tile_kernel_generated_1_t_kernel(tc, x, w1, w2, grad_out, out):
             + [i_eu(u) for u in V_OUT if u > 1],
         }
 
-        frees = {"d": "ed", "t": "et", "u": "eu"}
+        frees = {"d": "ed", "t": "et", "u": "eu", "x": "x"}
         done = set()
         filled = []
         heads = {q: 0 for q in queues}

from contextlib import ExitStack

import concourse.masks as masks
import concourse.mybir as mybir

FLOPS = 2 * 2048 * 3072 * 512
BYTES = 512 * 2 * 2 + 1024 * 3 * 512 * 2 + 2 * 512 * 1024 * 2 + 2 * 32768 * 32 * 4

F32 = mybir.dt.float32
BF16 = mybir.dt.bfloat16
U32 = mybir.dt.uint32
I32 = mybir.dt.int32
U8 = mybir.dt.uint8
E4M3 = mybir.dt.float8_e4m3fn_x4
E5M2 = mybir.dt.float8_e5m2_x4
MULT = mybir.AluOpType.mult
ADD = mybir.AluOpType.add
COPY = mybir.ActivationFunctionType.Copy

P = 128
S_TMP = ()
V_OUT = (1, 26, 28, 30)


def tile_kernel_generated_1_t_kernel(tc, x, w1, w2, grad_out, out):
    nc = tc.nc
    with ExitStack() as ctx:
        keep = ctx.enter_context(tc.tile_pool(name="keep", bufs=1))
        outs = ctx.enter_context(tc.tile_pool(name="outs", bufs=8))
        psum = ctx.enter_context(tc.psum_pool(name="psum", bufs=8))

        g_sb = [keep.tile([P, 4, 1088], BF16, name="g_sb%d" % m) for m in range(2)]
        w2_sb = keep.tile([P, 12288], BF16, name="w2_sb")
        w1_bf = keep.tile([P, 8], BF16, name="w1_bf")
        w1_f = keep.tile([P, 8], F32, name="w1_f")
        ident_f = keep.tile([P, P], F32, name="ident_f")
        ident_b = keep.tile([P, P], BF16, name="ident_b")
        diag = keep.tile([P, 8, P], BF16, name="diag")
        dg = [keep.tile([P, 2048], BF16, name="dg%d" % c, align_bytes=64) for c in range(4)]
        dc = keep.tile([P, 4 * 544], U32, name="dc", align_bytes=64)
        sp = keep.tile([P, 4 * 1536], U8, name="sp", align_bytes=64)
        wg = keep.tile([P, 12288], BF16, name="wg", align_bytes=64)
        wc = keep.tile([P, 3072], U32, name="wc", align_bytes=64)
        ws = keep.tile([P, 3072], U8, name="ws", align_bytes=64)
        tmp = {c: keep.tile([P, 4, 512], F32, name="tmp%d" % c) for c in (1, 2, 3)}
        dn = {c: keep.tile([P, 4, 512], BF16, name="dn%d" % c) for c in (1, 2, 3)}

        w2_f = w2_sb[:].bitcast(F32)
        wg_f = wg[:].bitcast(F32)
        banks = {}

        def evac(eng, dst, src):
            if eng == "v":
                nc.vector.tensor_copy(out=dst, in_=src)
            else:
                nc.scalar.copy(out=dst, in_=src)

        def load_g(m, l0, l1):
            for u in range(2):
                nc.sync.dma_start(
                    out=g_sb[m][:, 2 * u : 2 * u + 2, 32 * l0 : 32 * l1],
                    in_=grad_out[m, 256 * u : 256 * u + 256, l0:l1].rearrange("(p e) l n -> p e (l n)", e=2),
                )

        def load_w2(jp):
            nc.sync.dma_start(
                out=w2_sb[:, 3072 * jp : 3072 * jp + 3072].rearrange("j (a c) -> j a c", a=2),
                in_=w2[256 * jp : 256 * jp + 256].rearrange("(a j) k i -> j a (k i)", a=2),
            )

        def wrap_g(m):
            nc.vector.tensor_copy(out=g_sb[m][:, :, 1024:1088], in_=g_sb[m][:, :, 0:64])

        def d_pe(c, b):
            m, lh = divmod(c, 2)
            bank = psum.tile([P, 4, 128], F32, name="dbank", tag="bank")
            for t in range(4):
                for s in range(2):
                    c0 = (16 * lh + 4 * b + 1 + s) * 32
                    nc.tensor.matmul(
                        out=bank[:, t, :],
                        lhsT=diag[:, 2 * t + s, :],
                        rhs=g_sb[m][:, t, c0 : c0 + 128],
                        start=(s == 0),
                        stop=(s == 1),
                    )
            banks[("D", c, b)] = bank

        def d_ev(c, b, eng):
            dg4 = dg[c][:].rearrange("p (n l t) -> p n l t", n=32, l=16)
            evac(eng, dg4[:, :, 4 * b : 4 * b + 4, :], banks[("D", c, b)][:].rearrange("p t (l n) -> p n l t", l=4))

        def d_tmp(c, t, eng):
            m, lh = divmod(c, 2)
            c0 = (16 * lh + 2) * 32
            if eng == "s":
                nc.scalar.activation(
                    out=tmp[c][:, t, :], in_=g_sb[m][:, t, c0 : c0 + 512], func=COPY, scale=w1_f[:, 2 * t + 1 : 2 * t + 2]
                )
            else:
                nc.vector.tensor_scalar(
                    out=tmp[c][:, t, :],
                    in0=g_sb[m][:, t, c0 : c0 + 512],
                    scalar1=w1_f[:, 2 * t + 1 : 2 * t + 2],
                    scalar2=None,
                    op0=MULT,
                )

        def d_sum(c, t):
            m, lh = divmod(c, 2)
            c0 = (16 * lh + 1) * 32
            nc.vector.scalar_tensor_tensor(
                out=dn[c][:, t, :],
                in0=g_sb[m][:, t, c0 : c0 + 512],
                scalar=w1_f[:, 2 * t : 2 * t + 1],
                in1=tmp[c][:, t, :],
                op0=MULT,
                op1=ADD,
            )

        def d_regroup(c, half):
            dst = dg[c][:].rearrange("p (q i l t) -> p q l t i", q=8, i=4, l=16)
            src = dn[c][:].rearrange("p t (l q i) -> p q l t i", l=16, q=8)
            nc.vector.tensor_copy(out=dst[:, 4 * half : 4 * half + 4], in_=src[:, 4 * half : 4 * half + 4])

        def quant_d(c):
            nc.vector.quantize_mx(
                out=dc[:, 544 * c + 16 : 544 * c + 528].bitcast(E5M2),
                scales=sp[:, 1536 * c + 512 : 1536 * c + 1024],
                in_=dg[c][:],
            )

        def planes(c):
            b0 = 1536 * c
            nc.vector.tensor_copy(
                out=sp[:, b0 : b0 + 496].bitcast(I32), in_=sp[:, b0 + 528 : b0 + 1024].bitcast(I32)
            )
            nc.vector.tensor_copy(
                out=sp[:, b0 + 1040 : b0 + 1536].bitcast(I32), in_=sp[:, b0 + 512 : b0 + 1008].bitcast(I32)
            )

        def t_pe(c0):
            bank = psum.tile([P, 2, 2, 128], F32, name="xbank", tag="bank")
            for cc in range(2):
                for u in range(2):
                    w0 = 256 * (c0 + cc) + 128 * u
                    nc.tensor.transpose(bank[:, cc, u, :], w2_f[:, w0 : w0 + 128], ident_f[:])
            banks[("T", c0)] = bank

        def t_ev(c0, eng):
            evac(
                eng,
                wg_f[:, 256 * c0 : 256 * c0 + 512].rearrange("p (c j u) -> p c j u", c=2, u=2),
                banks[("T", c0)][:].rearrange("p c u j -> p c j u"),
            )

        def quant_w(c0, n):
            nc.vector.quantize_mx(
                out=wc[:, 128 * c0 : 128 * (c0 + n)].bitcast(E4M3),
                scales=ws[:, 128 * c0 : 128 * (c0 + n)],
                in_=wg[:, 512 * c0 : 512 * (c0 + n)],
            )

        def unit_pe(c, jt):
            acc = psum.tile([P, 512], F32, name="acc", tag="bank")
            for idx, k in enumerate((1, 0, 2)):
                wcol = (3 * jt + k) * 128
                col = 544 * c + 16 * (2 - k)
                nc.tensor.matmul_mx(
                    out=acc[:],
                    lhsT=wc[:, wcol : wcol + 128].bitcast(E4M3),
                    lhsT_scale=ws[:, wcol : wcol + 128],
                    rhs=dc[:, col : col + 512].bitcast(E5M2),
                    rhs_scale=sp[:, 1536 * c + 512 * k : 1536 * c + 512 * k + 512],
                    start=(idx == 0),
                    stop=(idx == 2),
                )
            banks[("U", c, jt)] = acc

        def warm_pe():
            bank = psum.tile([P, 512], F32, name="warm", tag="bank")
            for i in range(2):
                nc.tensor.matmul(out=bank[:], lhsT=ident_b[:], rhs=g_sb[0][:, i, 0:512], start=True, stop=True)

        def unit_ev(c, jt, eng, cuts):
            m, lh = divmod(c, 2)
            acc = banks[("U", c, jt)]
            o_sb = outs.tile([P, 512], F32, name="o_sb")
            o3 = o_sb[:].rearrange("j (l p) -> j l p", p=32)
            a3 = acc[:].rearrange("j (p l) -> j l p", l=16)
            o_dram = out[m, 4096 * jt : 4096 * jt + 4096, :].rearrange("(j l) p -> j (l p)", l=32)
            nl = 16 // cuts
            for cut in range(cuts):
                evac(eng, o3[:, nl * cut : nl * (cut + 1), :], a3[:, nl * cut : nl * (cut + 1), :])
                nc.sync.dma_start(
                    out=o_dram[:, 512 * lh + 32 * nl * cut : 512 * lh + 32 * nl * (cut + 1)],
                    in_=o_sb[:, 32 * nl * cut : 32 * nl * (cut + 1)],
                )

        ctx.enter_context(tc.manual_schedule())

        nc.scalar.dma_start(
            out=w1_bf[:].rearrange("p (u c) -> p u c", u=2),
            in_=w1.rearrange("(u p e) s -> p u (e s)", u=2, e=2),
        )
        load_g(0, 0, 10)
        load_g(0, 10, 18)
        load_g(0, 18, 32)
        load_w2(0)
        load_w2(1)
        load_w2(2)
        load_w2(3)
        load_g(1, 0, 18)
        load_g(1, 18, 32)

        nc.vector.memset(sp[:].bitcast(I32), 0)
        dc_i = dc[:].bitcast(I32).rearrange("p (c w) -> p c w", c=4)
        nc.vector.memset(dc_i[:, :, 0:16], 0)
        nc.vector.memset(dc_i[:, :, 528:544], 0)
        masks.make_identity(nc, ident_f[:])
        nc.vector.tensor_copy(out=ident_b[:], in_=ident_f[:])
        nc.vector.tensor_copy(out=w1_f[:], in_=w1_bf[:])
        for c in range(8):
            nc.vector.tensor_scalar(
                out=diag[:, c, :], in0=ident_b[:], scalar1=w1_f[:, c : c + 1], scalar2=None, op0=MULT
            )

        def tmp_on(c, t):
            return "s" if (c, t) in S_TMP else "v"

        def i_tmp(c, t):
            return (("tmp", c, t), (("wrap", c // 2),) if c % 2 else (), lambda: d_tmp(c, t, tmp_on(c, t)))

        def i_sum(c, t):
            return (("sum", c, t), (("tmp", c, t),), lambda: d_sum(c, t))

        def i_rg(c, half):
            return (("rg", c, half), tuple(("sum", c, t) for t in range(4)), lambda: d_regroup(c, half))

        def i_qd(c):
            need = tuple(("ed", b) for b in range(4)) if c == 0 else (("rg", c, 0), ("rg", c, 1))
            return (("qd", c), need, lambda: quant_d(c))

        def i_pl(c):
            return (("pl", c), (("qd", c),), lambda: planes(c))

        def i_qw(c0, n):
            return (("qw", c0), tuple(("et", e) for e in range(c0 - c0 % 2, c0 + n, 2)), lambda: quant_w(c0, n))

        def i_wrap(m):
            return (("wrap", m), (), lambda: wrap_g(m))

        def i_d(b):
            return (("d", b), (), lambda: d_pe(0, b))

        def i_ed(b, eng):
            return (("ed", b), (("d", b),), lambda: d_ev(0, b, eng))

        def i_t(c0):
            return (("t", c0), (), lambda: t_pe(c0))

        def i_et(c0, eng):
            return (("et", c0), (("t", c0),), lambda: t_ev(c0, eng))

        def i_u(u):
            c, jt = divmod(u, 8)
            return (("u", u), (("pl", c), ("qw", 6 * (jt // 2)), ("qw", 6 * (jt // 2) + 4)), lambda: unit_pe(c, jt))

        def i_x(n):
            return (("x", n), (), warm_pe)

        def i_eu(u):
            eng = "v" if u in V_OUT else "s"
            return (("eu", u), (("u", u),), lambda: unit_ev(u // 8, u % 8, eng, 2 if u == 31 else 1))

        def front(c):
            order = ((0, 0), (0, 1), (1, 0), (0, 2), (1, 1), (0, 3), (1, 2), (1, 3))
            return [(i_sum(c, t) if kind else i_tmp(c, t)) for kind, t in order if kind or tmp_on(c, t) == "v"]

        def qw_pair(jp):
            return [i_qw(6 * jp, 4), i_qw(6 * jp + 4, 2)]

        def weave(a, b):
            both = []
            for i in range(max(len(a), len(b))):
                both.extend(a[i : i + 1])
                both.extend(b[i : i + 1])
            return both

        queues = {
            "pe": [i_d(b) for b in range(4)]
            + [i_x(0)]
            + [i_t(c0) for c0 in (0, 2, 4)]
            + [i_x(1)]
            + [i_t(c0) for c0 in (6, 8, 10)]
            + [i_u(0)]
            + [i_t(c0) for c0 in (12, 14, 16)]
            + [i_u(1)]
            + [i_t(c0) for c0 in (18, 20, 22)]
            + [i_u(u) for u in range(2, 32)],
            "s": [i_ed(b, "s") for b in range(4)]
            + [i_et(c0, "s") for c0 in (0, 2, 4, 6, 8, 10, 12, 14, 16)]
            + [i_eu(0)]
            + [i_et(c0, "s") for c0 in (18, 20, 22)]
            + [i_eu(u) for u in range(2, 32) if u not in V_OUT],
            "v": [i_wrap(0)]
            + front(1)[0:4]
            + [i_qd(0), front(1)[4], i_pl(0), front(1)[5]]
            + qw_pair(0)
            + front(1)[6:8]
            + qw_pair(1)
            + [i_rg(1, 0)]
            + qw_pair(2)
            + [i_eu(1), i_rg(1, 1)]
            + qw_pair(3)
            + [i_qd(1), i_wrap(1), i_pl(1)]
            + front(2)
            + [i_rg(2, 0), i_rg(2, 1), front(3)[0], i_qd(2), front(3)[1], i_pl(2)]
            + front(3)[2:8]
            + [i_rg(3, 0), i_rg(3, 1), i_qd(3), i_pl(3)]
            + [i_eu(u) for u in V_OUT if u > 1],
        }

        frees = {"d": "ed", "t": "et", "u": "eu", "x": "x"}
        done = set()
        filled = []
        heads = {q: 0 for q in queues}
        left = sum(len(queues[q]) for q in queues)
        while left:
            moved = 0
            for q in ("pe", "s", "v"):
                if heads[q] >= len(queues[q]):
                    continue
                label, needs, call = queues[q][heads[q]]
                if any(need not in done for need in needs):
                    continue
                if q == "pe":
                    if len(filled) >= 8 and filled[len(filled) - 8] not in done:
                        continue
                    filled.append((frees[label[0]],) + tuple(label[1:]))
                call()
                done.add(label)
                heads[q] = heads[q] + 1
                moved = moved + 1
            assert moved, "the three orders wait for each other"
            left = left - moved
